import numpy as np
import ml_dtypes

BF16 = ml_dtypes.bfloat16


def bf(x):
    return np.asarray(x, np.float32).astype(BF16)


def f32(x):
    return np.asarray(x, np.float32)


def f64(x):
    return np.asarray(x).astype(np.float64)


def striped(idx):
    return np.tile(idx.reshape(-1, 16).T, (8, 1))


K, C, S, M, N = 4, 1024, 256, 256, 1024


def setup_inputs():
    return {"x": f32(np.random.standard_normal((K, C, S))), "offs": striped(np.concatenate([np.random.permutation(S) for _ in range(-(-(N) // S))])[:N])}


def reference(x, offs):
    idx = offs[:16].T.reshape(-1)
    x = f64(x)
    acc = np.zeros((C, M))
    for q in range(K):
        acc = acc + x[q][:, idx[q * M:(q + 1) * M]]
    return acc

@@ -1,0 +1,59 @@
+import concourse.mybir as mybir
+
+F32 = mybir.dt.float32
+U16 = mybir.dt.uint16
+ADD = mybir.AluOpType.add
+
+P = 128
+CELLS = 4
+POSITIONS = 1024
+CHANNELS = 256
+BLOCKS = POSITIONS // P
+PIECE_COLS = CHANNELS // 16
+SIDE_BY_SIDE = 2
+WARM = 64
+
+
+def tile_convproduct_kernel(tc, x, offs, out):
+    nc = tc.nc
+    with (
+        tc.tile_pool(name="held", bufs=1) as held,
+        tc.tile_pool(name="windows", bufs=CELLS * BLOCKS) as windows,
+        tc.tile_pool(name="sums", bufs=2 * BLOCKS) as sums,
+    ):
+        offsets = held.tile([P, CELLS * PIECE_COLS], U16, name="offsets")
+        nc.sync.dma_start(offsets[:], offs)
+
+        window = {}
+        for pair in range(0, BLOCKS, SIDE_BY_SIDE):
+            for q in range(CELLS):
+                for b in range(pair, pair + SIDE_BY_SIDE):
+                    window[q, b] = windows.tile([P, CHANNELS], F32, name="window")
+                    queue = nc.scalar if b % 2 == 0 else nc.sync
+                    queue.dma_start(window[q, b][:], x[q, b * P : (b + 1) * P, :])
+
+        zeros = held.tile([P, WARM], F32, name="zeros")
+        copied = held.tile([P, WARM], F32, name="copied")
+        added = held.tile([P, WARM], F32, name="added")
+        nc.vector.memset(zeros[:], 0.0)
+        nc.vector.tensor_copy(copied[:], zeros[:])
+        nc.vector.tensor_tensor(added[:], zeros[:], copied[:], ADD)
+
+        total = {}
+        for pair in range(0, BLOCKS, SIDE_BY_SIDE):
+            for q in range(CELLS):
+                for b in range(pair, pair + SIDE_BY_SIDE):
+                    longer = sums.tile([P, CHANNELS], F32, name="longer")
+                    parts = 2 if (q, b) == (CELLS - 1, BLOCKS - 1) else 1
+                    width = CHANNELS // parts
+                    for h in range(parts):
+                        columns = slice(h * width, (h + 1) * width)
+                        first = q * PIECE_COLS + h * width // 16
+                        picked = window[q, b][:].indirect(offsets[:, first : first + width // 16])
+                        if q == 0:
+                            nc.vector.tensor_copy(longer[:, columns], picked)
+                        else:
+                            nc.vector.tensor_tensor(longer[:, columns], picked, total[b][:, columns], ADD)
+                        if q == CELLS - 1:
+                            nc.sync.dma_start(out[b * P : (b + 1) * P, columns], longer[:, columns])
+                    total[b] = longer

@@ -24,13 +24,15 @@ def tile_convproduct_kernel(tc, x, offs, out):
         offsets = held.tile([P, CELLS * PIECE_COLS], U16, name="offsets")
         nc.sync.dma_start(offsets[:], offs)
 
+        x_blocks = x.rearrange("q (p b) c -> q b p c", b=BLOCKS)
+        out_blocks = out.rearrange("(p b) c -> b p c", b=BLOCKS)
         window = {}
         for pair in range(0, BLOCKS, SIDE_BY_SIDE):
             for q in range(CELLS):
                 for b in range(pair, pair + SIDE_BY_SIDE):
                     window[q, b] = windows.tile([P, CHANNELS], F32, name="window")
                     queue = nc.scalar if b % 2 == 0 else nc.sync
-                    queue.dma_start(window[q, b][:], x[q, b * P : (b + 1) * P, :])
+                    queue.dma_start(window[q, b][:], x_blocks[q, b])
 
         zeros = held.tile([P, WARM], F32, name="zeros")
         copied = held.tile([P, WARM], F32, name="copied")
@@ -55,5 +57,5 @@ def tile_convproduct_kernel(tc, x, offs, out):
                         else:
                             nc.vector.tensor_tensor(longer[:, columns], picked, total[b][:, columns], ADD)
                         if q == CELLS - 1:
-                            nc.sync.dma_start(out[b * P : (b + 1) * P, columns], longer[:, columns])
+                            nc.sync.dma_start(out_blocks[b, :, columns], longer[:, columns])
                     total[b] = longer

import concourse.mybir as mybir

F32 = mybir.dt.float32
U16 = mybir.dt.uint16
ADD = mybir.AluOpType.add

P = 128
CELLS = 4
POSITIONS = 1024
CHANNELS = 256
BLOCKS = POSITIONS // P
PIECE_COLS = CHANNELS // 16
SIDE_BY_SIDE = 2
WARM = 64


def tile_convproduct_kernel(tc, x, offs, out):
    nc = tc.nc
    with (
        tc.tile_pool(name="held", bufs=1) as held,
        tc.tile_pool(name="windows", bufs=CELLS * BLOCKS) as windows,
        tc.tile_pool(name="sums", bufs=2 * BLOCKS) as sums,
    ):
        offsets = held.tile([P, CELLS * PIECE_COLS], U16, name="offsets")
        nc.sync.dma_start(offsets[:], offs)

        x_blocks = x.rearrange("q (p b) c -> q b p c", b=BLOCKS)
        out_blocks = out.rearrange("(p b) c -> b p c", b=BLOCKS)
        window = {}
        for pair in range(0, BLOCKS, SIDE_BY_SIDE):
            for q in range(CELLS):
                for b in range(pair, pair + SIDE_BY_SIDE):
                    window[q, b] = windows.tile([P, CHANNELS], F32, name="window")
                    queue = nc.scalar if b % 2 == 0 else nc.sync
                    queue.dma_start(window[q, b][:], x_blocks[q, b])

        zeros = held.tile([P, WARM], F32, name="zeros")
        copied = held.tile([P, WARM], F32, name="copied")
        added = held.tile([P, WARM], F32, name="added")
        nc.vector.memset(zeros[:], 0.0)
        nc.vector.tensor_copy(copied[:], zeros[:])
        nc.vector.tensor_tensor(added[:], zeros[:], copied[:], ADD)

        total = {}
        for pair in range(0, BLOCKS, SIDE_BY_SIDE):
            for q in range(CELLS):
                for b in range(pair, pair + SIDE_BY_SIDE):
                    longer = sums.tile([P, CHANNELS], F32, name="longer")
                    parts = 2 if (q, b) == (CELLS - 1, BLOCKS - 1) else 1
                    width = CHANNELS // parts
                    for h in range(parts):
                        columns = slice(h * width, (h + 1) * width)
                        first = q * PIECE_COLS + h * width // 16
                        picked = window[q, b][:].indirect(offsets[:, first : first + width // 16])
                        if q == 0:
                            nc.vector.tensor_copy(longer[:, columns], picked)
                        else:
                            nc.vector.tensor_tensor(longer[:, columns], picked, total[b][:, columns], ADD)
                        if q == CELLS - 1:
                            nc.sync.dma_start(out_blocks[b, :, columns], longer[:, columns])
                    total[b] = longer
